import numpy as np
import ml_dtypes

BF16 = ml_dtypes.bfloat16


def bf(x):
    return np.asarray(x, np.float32).astype(BF16)


def f32(x):
    return np.asarray(x, np.float32)


def f64(x):
    return np.asarray(x).astype(np.float64)


def striped(idx):
    return np.tile(idx.reshape(-1, 16).T, (8, 1))


V, D, H, HD, N = 2048, 512, 4, 128, 1024
EPS = 1e-5


def weight(scale):
    return bf(scale * np.random.standard_normal((D, D)) / np.sqrt(D))


def column(scale):
    return f32(scale * np.random.standard_normal((D, 1)))


def setup_inputs():
    return {
        'emb': f32(np.random.standard_normal((D, V))),
        'pos': f32(0.5 * np.random.standard_normal((D, N))),
        'wq': weight(1.2),
        'wk': weight(1.2),
        'wv': weight(2.0),
        'wo': weight(1.0),
        'bq': column(0.2),
        'bv': column(0.1),
        'bo': column(0.1),
        'gain': f32(1.0 + 0.1 * np.random.standard_normal((D, 1))),
        'shift': column(0.1),
        'offs': striped(np.random.permutation(np.tile(np.arange(V), 2))[:N]),
    }


def reference(emb, pos, wq, wk, wv, wo, bq, bv, bo, gain, shift, offs):
    idx = offs[:16].T.reshape(-1)
    x = f64(emb)[:, idx] + f64(pos)
    q = f64(wq).T @ x + f64(bq)
    k = f64(wk).T @ x
    v = f64(wv).T @ x + f64(bv)
    keep = np.arange(N)[:, None] <= np.arange(N)[None, :]
    o = np.zeros((D, N), np.float64)
    for h in range(H):
        r = slice(h * HD, (h + 1) * HD)
        sc = k[r].T @ q[r] / np.sqrt(HD)
        sc = np.where(keep, sc, -np.inf)
        e = np.exp(sc - sc.max(axis=0, keepdims=True))
        a = e / e.sum(axis=0, keepdims=True)
        o[r] = v[r] @ a
    y = x + f64(wo).T @ o + f64(bo)
    mu = y.mean(axis=0, keepdims=True)
    var = ((y - mu) ** 2).mean(axis=0, keepdims=True)
    return (y - mu) / np.sqrt(var + EPS) * f64(gain) + f64(shift)

@@ -1,0 +1,324 @@
+import math
+
+import concourse.mybir as mybir
+from concourse.masks import make_identity
+
+F32 = mybir.dt.float32
+BF16 = mybir.dt.bfloat16
+U16 = mybir.dt.uint16
+ALU = mybir.AluOpType
+ACT = mybir.ActivationFunctionType
+AXIS = mybir.AxisListType
+
+P = 128
+D, V, N, H = 512, 2048, 1024, 4
+CB = D // P
+TB = N // P
+BANK = 512
+HALVES = N // BANK
+EPS = 1e-5
+MASKED = -1e30
+
+FLOPS = 4 * 2 * D * D * N + 2 * 2 * D * (N * (N + 1) // 2)
+
+
+def tile_sequencedecodermoe_b_kernel(
+    tc, emb, pos, wq, wk, wv, wo, bq, bv, bo, gain, shift, offs, out
+):
+    nc = tc.nc
+    with (
+        tc.tile_pool(name="held", bufs=1) as held,
+        tc.tile_pool(name="ring", bufs=3) as ring,
+        tc.tile_pool(name="small", bufs=8) as small,
+        tc.tile_pool(name="norm", bufs=2) as norm,
+        tc.psum_pool(name="psum", bufs=8) as psum,
+    ):
+
+        def new_bank():
+            return psum.tile([P, BANK], F32, name="bank", tag="bank")
+
+        offsets = held.tile([P, N // 16], U16, name="offsets")
+        nc.sync.dma_start(offsets[:], offs)
+
+        emb_sb, pos_sb = [], []
+        for c in range(CB):
+            emb_c = held.tile([P, V], F32, name=f"emb{c}")
+            nc.sync.dma_start(emb_c[:], emb[c * P : (c + 1) * P, :])
+            emb_sb.append(emb_c)
+            pos_c = held.tile([P, N], F32, name=f"pos{c}")
+            nc.scalar.dma_start(pos_c[:], pos[c * P : (c + 1) * P, :])
+            pos_sb.append(pos_c)
+
+        def load_weight(w, name):
+            w_sb = held.tile([P, CB, D], BF16, name=name)
+            nc.gpsimd.dma_start(w_sb[:], w.rearrange("(a p) e -> p a e", p=P))
+            return w_sb
+
+        wq_sb = load_weight(wq, "wq_sb")
+        wk_sb = load_weight(wk, "wk_sb")
+        wv_sb = load_weight(wv, "wv_sb")
+        wo_sb = load_weight(wo, "wo_sb")
+
+        def load_column(b, name):
+            b_sb = held.tile([P, CB], F32, name=name)
+            with nc.allow_non_contiguous_dma(reason="one value to a partition"):
+                nc.scalar.dma_start(b_sb[:], b.rearrange("(a p) o -> p (a o)", p=P))
+            return b_sb
+
+        bq_sb = load_column(bq, "bq_sb")
+        bv_sb = load_column(bv, "bv_sb")
+        bo_sb = load_column(bo, "bo_sb")
+        gain_sb = load_column(gain, "gain_sb")
+        shift_sb = load_column(shift, "shift_sb")
+
+        ident = held.tile([P, P], BF16, name="ident")
+        make_identity(nc, ident[:])
+        mask = held.tile([P, P], BF16, name="mask")
+        nc.gpsimd.memset(mask[:], 0.0)
+        nc.gpsimd.affine_select(
+            out=mask[:],
+            in_=mask[:],
+            pattern=[[-1, P]],
+            compare_op=ALU.is_ge,
+            fill=MASKED,
+            base=0,
+            channel_multiplier=1,
+        )
+        averager = held.tile([P, P], BF16, name="averager")
+        nc.gpsimd.memset(averager[:], 1.0 / D)
+        eps_col = held.tile([P, 1], F32, name="eps_col")
+        nc.gpsimd.memset(eps_col[:], EPS)
+
+        x, x_bf = [], []
+        for c in range(CB):
+            x_c = held.tile([P, N], F32, name=f"x{c}")
+            nc.vector.tensor_tensor(
+                x_c[:], emb_sb[c][:].indirect(offsets[:]), pos_sb[c][:], ALU.add
+            )
+            x.append(x_c)
+            x_bf_c = held.tile([P, N], BF16, name=f"x_bf{c}")
+            nc.scalar.copy(x_bf_c[:], x_c[:])
+            x_bf.append(x_bf_c)
+
+        q_ps = [[new_bank() for half in range(HALVES)] for h in range(H)]
+        for c in range(CB):
+            for h in range(H):
+                for half in range(HALVES):
+                    nc.tensor.matmul(
+                        q_ps[h][half][:],
+                        lhsT=wq_sb[:, c, h * P : (h + 1) * P],
+                        rhs=x_bf[c][:, half * BANK : (half + 1) * BANK],
+                        start=(c == 0),
+                        stop=(c == CB - 1),
+                    )
+        q_bf = []
+        for h in range(H):
+            q_h = held.tile([P, N], BF16, name=f"q{h}")
+            for half in range(HALVES):
+                nc.vector.tensor_scalar(
+                    out=q_h[:, half * BANK : (half + 1) * BANK],
+                    in0=q_ps[h][half][:],
+                    scalar1=bq_sb[:, h : h + 1],
+                    scalar2=1.0 / math.sqrt(P),
+                    op0=ALU.add,
+                    op1=ALU.mult,
+                )
+            q_bf.append(q_h)
+
+        k_bf = []
+        for h in range(H):
+            k_h = held.tile([P, N], BF16, name=f"k{h}")
+            for half in range(HALVES):
+                k_ps = new_bank()
+                for c in range(CB):
+                    nc.tensor.matmul(
+                        k_ps[:],
+                        lhsT=wk_sb[:, c, h * P : (h + 1) * P],
+                        rhs=x_bf[c][:, half * BANK : (half + 1) * BANK],
+                        start=(c == 0),
+                        stop=(c == CB - 1),
+                    )
+                nc.scalar.copy(k_h[:, half * BANK : (half + 1) * BANK], k_ps[:])
+            k_bf.append(k_h)
+
+        v_t = []
+        for tb in range(TB):
+            v_ps = new_bank()
+            for c in range(CB):
+                nc.tensor.matmul(
+                    v_ps[:],
+                    lhsT=x_bf[c][:, tb * P : (tb + 1) * P],
+                    rhs=wv_sb[:, c, :],
+                    start=(c == 0),
+                    stop=(c == CB - 1),
+                )
+            v_tb = held.tile([P, D], BF16, name=f"v_t{tb}")
+            if tb % 2 == 0:
+                nc.vector.tensor_copy(v_tb[:], v_ps[:])
+            else:
+                nc.scalar.copy(v_tb[:], v_ps[:])
+            v_t.append(v_tb)
+
+        o_bf = [held.tile([P, N], BF16, name=f"o{h}") for h in range(H)]
+
+        def attend(jb, h):
+            keys = (jb + 1) * P
+            queries = slice(jb * P, keys)
+            starts = list(range(0, keys, BANK))
+
+            score = []
+            for a in starts:
+                b = min(a + BANK, keys)
+                s_ps = new_bank()
+                past = min(b, jb * P)
+                if past > a:
+                    nc.tensor.matmul(
+                        s_ps[:, 0 : past - a],
+                        lhsT=q_bf[h][:, queries],
+                        rhs=k_bf[h][:, a:past],
+                        start=True,
+                        stop=True,
+                    )
+                if b == keys:
+                    own = s_ps[:, jb * P - a : keys - a]
+                    nc.tensor.matmul(
+                        own, lhsT=q_bf[h][:, queries], rhs=k_bf[h][:, queries],
+                        start=True, stop=False,
+                    )
+                    nc.tensor.matmul(own, lhsT=ident[:], rhs=mask[:], start=False, stop=True)
+                score.append(s_ps)
+
+            neg_max_parts = small.tile([P, 2], F32, name="neg_max_parts")
+            for i, a in enumerate(starts):
+                nc.vector.tensor_reduce(
+                    out=neg_max_parts[:, i : i + 1],
+                    in_=score[i][:, 0 : min(BANK, keys - a)],
+                    axis=AXIS.X,
+                    op=ALU.max,
+                    negate=True,
+                )
+            if len(starts) == 2:
+                neg_max = small.tile([P, 1], F32, name="neg_max")
+                nc.vector.tensor_tensor(
+                    neg_max[:], neg_max_parts[:, 0:1], neg_max_parts[:, 1:2], ALU.min
+                )
+            else:
+                neg_max = neg_max_parts
+
+            prob = ring.tile([P, N], BF16, name="prob")
+            sum_parts = small.tile([P, 2], F32, name="sum_parts")
+            for i, a in enumerate(starts):
+                b = min(a + BANK, keys)
+                nc.scalar.activation(
+                    out=prob[:, a:b],
+                    in_=score[i][:, 0 : b - a],
+                    func=ACT.Exp,
+                    bias=neg_max[:, 0:1],
+                    scale=1.0,
+                    accum_out=sum_parts[:, i : i + 1],
+                )
+            if len(starts) == 2:
+                total = small.tile([P, 1], F32, name="total")
+                nc.vector.tensor_tensor(total[:], sum_parts[:, 0:1], sum_parts[:, 1:2], ALU.add)
+            else:
+                total = sum_parts
+            recip = small.tile([P, 1], F32, name="recip")
+            nc.vector.reciprocal(recip[:], total[:, 0:1])
+
+            diag_r = ring.tile([P, P], BF16, name="diag_r")
+            nc.gpsimd.tensor_scalar(
+                out=diag_r[:], in0=ident[:], scalar1=recip[:, 0:1], scalar2=0.0,
+                op0=ALU.mult, op1=ALU.add,
+            )
+            weights_t = ring.tile([P, N], BF16, name="weights_t")
+            for a in starts:
+                b = min(a + BANK, keys)
+                t_ps = new_bank()
+                for tb in range(a // P, b // P):
+                    nc.tensor.matmul(
+                        t_ps[:, tb * P - a : (tb + 1) * P - a],
+                        lhsT=prob[:, tb * P : (tb + 1) * P],
+                        rhs=diag_r[:],
+                        start=True,
+                        stop=True,
+                    )
+                if h % 2 == 0:
+                    nc.vector.tensor_copy(weights_t[:, a:b], t_ps[:, 0 : b - a])
+                else:
+                    nc.scalar.copy(weights_t[:, a:b], t_ps[:, 0 : b - a])
+
+            o_ps = new_bank()
+            for tb in range(jb + 1):
+                nc.tensor.matmul(
+                    o_ps[:, 0:P],
+                    lhsT=v_t[tb][:, h * P : (h + 1) * P],
+                    rhs=weights_t[:, tb * P : (tb + 1) * P],
+                    start=(tb == 0),
+                    stop=(tb == jb),
+                )
+            nc.scalar.activation(
+                out=o_bf[h][:, queries], in_=o_ps[:, 0:P], func=ACT.Identity,
+                bias=bv_sb[:, h : h + 1], scale=1.0,
+            )
+
+        def finish(half):
+            cols = slice(half * BANK, (half + 1) * BANK)
+            y, y_bf = [], []
+            for eb in range(CB):
+                y_ps = new_bank()
+                for c in range(CB):
+                    nc.tensor.matmul(
+                        y_ps[:],
+                        lhsT=wo_sb[:, c, eb * P : (eb + 1) * P],
+                        rhs=o_bf[c][:, cols],
+                        start=(c == 0),
+                        stop=(c == CB - 1),
+                    )
+                y_eb = norm.tile([P, BANK], F32, name=f"y{eb}")
+                nc.vector.scalar_tensor_tensor(
+                    out=y_eb[:], in0=y_ps[:], scalar=bo_sb[:, eb : eb + 1], in1=x[eb][:, cols],
+                    op0=ALU.add, op1=ALU.add,
+                )
+                y.append(y_eb)
+                y_bf_eb = norm.tile([P, BANK], BF16, name=f"y_bf{eb}")
+                nc.gpsimd.tensor_scalar(
+                    out=y_bf_eb[:], in0=y_eb[:], scalar1=1.0, scalar2=0.0,
+                    op0=ALU.mult, op1=ALU.add,
+                )
+                y_bf.append(y_bf_eb)
+            mean_ps = new_bank()
+            for eb in range(CB):
+                nc.tensor.matmul(
+                    mean_ps[:], lhsT=averager[:], rhs=y_bf[eb][:],
+                    start=(eb == 0), stop=(eb == CB - 1),
+                )
+            var_ps = new_bank()
+            for eb in range(CB):
+                nc.vector.tensor_tensor(y[eb][:], y[eb][:], mean_ps[:], ALU.subtract)
+                sq_eb = norm.tile([P, BANK], BF16, name=f"sq{eb}")
+                nc.gpsimd.tensor_tensor(sq_eb[:], y[eb][:], y[eb][:], ALU.mult)
+                nc.tensor.matmul(
+                    var_ps[:], lhsT=averager[:], rhs=sq_eb[:],
+                    start=(eb == 0), stop=(eb == CB - 1),
+                )
+            rstd = norm.tile([P, BANK], F32, name="rstd")
+            nc.scalar.activation(
+                out=rstd[:], in_=var_ps[:], func=ACT.Abs_reciprocal_sqrt,
+                bias=eps_col[:, 0:1], scale=1.0,
+            )
+            for eb in range(CB):
+                nc.vector.scalar_tensor_tensor(
+                    out=y[eb][:], in0=y[eb][:], scalar=gain_sb[:, eb : eb + 1], in1=rstd[:],
+                    op0=ALU.mult, op1=ALU.mult,
+                )
+                nc.gpsimd.tensor_scalar(
+                    out=y[eb][:], in0=y[eb][:], scalar1=1.0, scalar2=shift_sb[:, eb : eb + 1],
+                    op0=ALU.mult, op1=ALU.add,
+                )
+                nc.sync.dma_start(out[eb * P : (eb + 1) * P, cols], y[eb][:])
+
+        for jb in range(TB):
+            for h in range(H):
+                attend(jb, h)
+            if (jb + 1) * P % BANK == 0:
+                finish((jb + 1) * P // BANK - 1)

@@ -19,6 +19,9 @@ HALVES = N // BANK
 EPS = 1e-5
 MASKED = -1e30
 
+EXP_LAG, FLIP_LAG, MIX_LAG, STORE_LAG = 1, 3, 5, 6
+PROJECT_LAG, DEVIATION_LAG, NORMALISE_LAG = 0, 2, 3
+
 FLOPS = 4 * 2 * D * D * N + 2 * 2 * D * (N * (N + 1) // 2)
 
 
@@ -28,46 +31,49 @@ def tile_sequencedecodermoe_b_kernel(
     nc = tc.nc
     with (
         tc.tile_pool(name="held", bufs=1) as held,
-        tc.tile_pool(name="ring", bufs=3) as ring,
+        tc.tile_pool(name="ring", bufs=6) as ring,
         tc.tile_pool(name="small", bufs=8) as small,
-        tc.tile_pool(name="norm", bufs=2) as norm,
+        tc.tile_pool(name="norm", bufs=3) as norm,
         tc.psum_pool(name="psum", bufs=8) as psum,
     ):
 
-        def new_bank():
-            return psum.tile([P, BANK], F32, name="bank", tag="bank")
+        def new_bank(dtype=F32, cols=BANK):
+            return psum.tile([P, cols], dtype, name="bank", tag="bank")
+
+        def half_cols(half):
+            return slice(half * BANK, (half + 1) * BANK)
+
+        def block_cols(b):
+            return slice(b * P, (b + 1) * P)
 
         offsets = held.tile([P, N // 16], U16, name="offsets")
         nc.sync.dma_start(offsets[:], offs)
 
-        emb_sb, pos_sb = [], []
-        for c in range(CB):
-            emb_c = held.tile([P, V], F32, name=f"emb{c}")
-            nc.sync.dma_start(emb_c[:], emb[c * P : (c + 1) * P, :])
-            emb_sb.append(emb_c)
-            pos_c = held.tile([P, N], F32, name=f"pos{c}")
-            nc.scalar.dma_start(pos_c[:], pos[c * P : (c + 1) * P, :])
-            pos_sb.append(pos_c)
-
-        def load_weight(w, name):
+        def load_weight(w, name, queue):
             w_sb = held.tile([P, CB, D], BF16, name=name)
-            nc.gpsimd.dma_start(w_sb[:], w.rearrange("(a p) e -> p a e", p=P))
+            queue.dma_start(w_sb[:], w.rearrange("(a p) e -> p a e", p=P))
             return w_sb
 
-        wq_sb = load_weight(wq, "wq_sb")
-        wk_sb = load_weight(wk, "wk_sb")
-        wv_sb = load_weight(wv, "wv_sb")
-        wo_sb = load_weight(wo, "wo_sb")
+        emb_sb = [held.tile([P, V], F32, name=f"emb{c}") for c in range(CB)]
+        pos_sb = [held.tile([P, N], F32, name=f"pos{c}") for c in range(CB)]
+        for c in range(CB):
+            nc.sync.dma_start(emb_sb[c][:], emb[block_cols(c), :])
+            nc.scalar.dma_start(pos_sb[c][:], pos[block_cols(c), :])
+            if c == 1:
+                wq_sb = load_weight(wq, "wq_sb", nc.scalar)
+        wk_sb = load_weight(wk, "wk_sb", nc.sync)
+        wv_sb = load_weight(wv, "wv_sb", nc.sync)
+        wo_sb = load_weight(wo, "wo_sb", nc.sync)
 
         def load_column(b, name):
             b_sb = held.tile([P, CB], F32, name=name)
             with nc.allow_non_contiguous_dma(reason="one value to a partition"):
-                nc.scalar.dma_start(b_sb[:], b.rearrange("(a p) o -> p (a o)", p=P))
+                nc.gpsimd.dma_start(b_sb[:], b.rearrange("(a p) o -> p (a o)", p=P))
             return b_sb
 
+        bo_sb = load_column(bo, "bo_sb")
         bq_sb = load_column(bq, "bq_sb")
         bv_sb = load_column(bv, "bv_sb")
-        bo_sb = load_column(bo, "bo_sb")
         gain_sb = load_column(gain, "gain_sb")
         shift_sb = load_column(shift, "shift_sb")
 
@@ -86,239 +92,293 @@ def tile_sequencedecodermoe_b_kernel(
         )
         averager = held.tile([P, P], BF16, name="averager")
         nc.gpsimd.memset(averager[:], 1.0 / D)
+        averager_f32 = held.tile([P, P], F32, name="averager_f32")
+        nc.gpsimd.memset(averager_f32[:], 1.0 / D)
         eps_col = held.tile([P, 1], F32, name="eps_col")
         nc.gpsimd.memset(eps_col[:], EPS)
 
-        x, x_bf = [], []
-        for c in range(CB):
-            x_c = held.tile([P, N], F32, name=f"x{c}")
-            nc.vector.tensor_tensor(
-                x_c[:], emb_sb[c][:].indirect(offsets[:]), pos_sb[c][:], ALU.add
-            )
-            x.append(x_c)
-            x_bf_c = held.tile([P, N], BF16, name=f"x_bf{c}")
-            nc.scalar.copy(x_bf_c[:], x_c[:])
-            x_bf.append(x_bf_c)
+        bo_mean_ps = new_bank()
+        nc.tensor.matmul(bo_mean_ps[:, 0:CB], lhsT=averager_f32[:], rhs=bo_sb[:], start=True, stop=True)
+        bo_mean = small.tile([P, 1], F32, name="bo_mean")
+        nc.vector.tensor_reduce(out=bo_mean[:], in_=bo_mean_ps[:, 0:CB], axis=AXIS.X, op=ALU.add)
+        bo_centred = held.tile([P, CB], F32, name="bo_centred")
+        nc.vector.tensor_scalar(
+            out=bo_centred[:], in0=bo_sb[:], scalar1=bo_mean[:, 0:1], scalar2=None, op0=ALU.subtract
+        )
 
+        bq_scaled = held.tile([P, CB], F32, name="bq_scaled")
+        nc.vector.tensor_scalar(
+            out=bq_scaled[:], in0=bq_sb[:], scalar1=1.0 / math.sqrt(P), scalar2=None, op0=ALU.mult
+        )
+
+        x = held.tile([P, CB, N], F32, name="x")
+        x_bf = held.tile([P, CB, N], BF16, name="x_bf")
         q_ps = [[new_bank() for half in range(HALVES)] for h in range(H)]
         for c in range(CB):
-            for h in range(H):
-                for half in range(HALVES):
+            for half in range(HALVES):
+                cols = half_cols(half)
+                nc.vector.tensor_tensor(
+                    x[:, c, cols],
+                    emb_sb[c][:].indirect(offsets[:, half * (BANK // 16) : (half + 1) * (BANK // 16)]),
+                    pos_sb[c][:, cols],
+                    ALU.add,
+                )
+                nc.scalar.copy(x_bf[:, c, cols], x[:, c, cols])
+                for h in range(H):
                     nc.tensor.matmul(
                         q_ps[h][half][:],
-                        lhsT=wq_sb[:, c, h * P : (h + 1) * P],
-                        rhs=x_bf[c][:, half * BANK : (half + 1) * BANK],
+                        lhsT=wq_sb[:, c, block_cols(h)],
+                        rhs=x_bf[:, c, cols],
                         start=(c == 0),
                         stop=(c == CB - 1),
                     )
-        q_bf = []
-        for h in range(H):
-            q_h = held.tile([P, N], BF16, name=f"q{h}")
-            for half in range(HALVES):
-                nc.vector.tensor_scalar(
-                    out=q_h[:, half * BANK : (half + 1) * BANK],
-                    in0=q_ps[h][half][:],
-                    scalar1=bq_sb[:, h : h + 1],
-                    scalar2=1.0 / math.sqrt(P),
-                    op0=ALU.add,
-                    op1=ALU.mult,
-                )
-            q_bf.append(q_h)
 
-        k_bf = []
+        for c in range(CB):
+            nc.gpsimd.tensor_scalar(
+                out=x[:, c, :], in0=x[:, c, :], scalar1=1.0, scalar2=bo_centred[:, c : c + 1],
+                op0=ALU.mult, op1=ALU.add,
+            )
+
+        q_bf = held.tile([P, H, N], BF16, name="q_bf")
         for h in range(H):
-            k_h = held.tile([P, N], BF16, name=f"k{h}")
-            for half in range(HALVES):
-                k_ps = new_bank()
+            nc.vector.tensor_scalar(
+                out=q_bf[:, h, half_cols(0)],
+                in0=q_ps[h][0][:],
+                scalar1=bq_sb[:, h : h + 1],
+                scalar2=1.0 / math.sqrt(P),
+                op0=ALU.add,
+                op1=ALU.mult,
+            )
+            nc.scalar.activation(
+                out=q_bf[:, h, half_cols(1)], in_=q_ps[h][1][:], func=ACT.Identity,
+                bias=bq_scaled[:, h : h + 1], scale=1.0 / math.sqrt(P),
+            )
+
+        wo_centred = held.tile([P, CB, D], BF16, name="wo_centred")
+
+        def centre_wo(c):
+            row_sum = small.tile([P, 1], F32, name="wo_row_sum")
+            nc.vector.tensor_reduce(out=row_sum[:], in_=wo_sb[:, c, :], axis=AXIS.X, op=ALU.add)
+            neg_mean = small.tile([P, 1], F32, name="wo_neg_mean")
+            nc.vector.tensor_scalar(
+                out=neg_mean[:], in0=row_sum[:], scalar1=-1.0 / D, scalar2=None, op0=ALU.mult
+            )
+            nc.gpsimd.tensor_scalar(
+                out=wo_centred[:, c, :], in0=wo_sb[:, c, :],
+                scalar1=1.0, scalar2=neg_mean[:, 0:1], op0=ALU.mult, op1=ALU.add,
+            )
+
+        k_bf = held.tile([P, H, N], BF16, name="k_bf")
+        v_t = [held.tile([P, D], BF16, name=f"v_t{tb}") for tb in range(TB)]
+
+        def project_k(tb, heads):
+            k_ps = new_bank()
+            for i, h in enumerate(heads):
                 for c in range(CB):
                     nc.tensor.matmul(
-                        k_ps[:],
-                        lhsT=wk_sb[:, c, h * P : (h + 1) * P],
-                        rhs=x_bf[c][:, half * BANK : (half + 1) * BANK],
-                        start=(c == 0),
-                        stop=(c == CB - 1),
+                        k_ps[:, block_cols(i)], lhsT=wk_sb[:, c, block_cols(h)], rhs=x_bf[:, c, block_cols(tb)],
+                        start=(c == 0), stop=(c == CB - 1),
                     )
-                nc.scalar.copy(k_h[:, half * BANK : (half + 1) * BANK], k_ps[:])
-            k_bf.append(k_h)
+            nc.scalar.copy(
+                k_bf[:, heads[0] : heads[-1] + 1, block_cols(tb)],
+                k_ps[:, 0 : len(heads) * P].rearrange("p (h t) -> p h t", t=P),
+            )
 
-        v_t = []
-        for tb in range(TB):
+        def project_v(tb):
             v_ps = new_bank()
             for c in range(CB):
                 nc.tensor.matmul(
-                    v_ps[:],
-                    lhsT=x_bf[c][:, tb * P : (tb + 1) * P],
-                    rhs=wv_sb[:, c, :],
-                    start=(c == 0),
-                    stop=(c == CB - 1),
+                    v_ps[:], lhsT=x_bf[:, c, block_cols(tb)], rhs=wv_sb[:, c, :],
+                    start=(c == 0), stop=(c == CB - 1),
                 )
-            v_tb = held.tile([P, D], BF16, name=f"v_t{tb}")
-            if tb % 2 == 0:
-                nc.vector.tensor_copy(v_tb[:], v_ps[:])
-            else:
-                nc.scalar.copy(v_tb[:], v_ps[:])
-            v_t.append(v_tb)
+            nc.scalar.copy(v_t[tb][:], v_ps[:])
 
-        o_bf = [held.tile([P, N], BF16, name=f"o{h}") for h in range(H)]
+        def centre_x(tb):
+            x_mean_ps = new_bank()
+            for c in range(CB):
+                nc.tensor.matmul(
+                    x_mean_ps[:, 0:P], lhsT=averager[:], rhs=x_bf[:, c, block_cols(tb)],
+                    start=(c == 0), stop=(c == CB - 1),
+                )
+            nc.vector.tensor_tensor(
+                x[:, :, block_cols(tb)],
+                x[:, :, block_cols(tb)],
+                x_mean_ps[:, 0:P].unsqueeze(1).to_broadcast([P, CB, P]),
+                ALU.subtract,
+            )
 
-        def attend(jb, h):
+        def prepare(tb, piece):
+            if piece == 0:
+                project_k(tb, [0, 1])
+            elif piece == 1:
+                project_k(tb, [2, 3])
+            elif piece == 2:
+                project_v(tb)
+
+        items = [(jb, h) for jb in range(TB) for h in range(H)]
+        n_items = len(items)
+        score_ps = [None] * n_items
+        neg_max = [None] * n_items
+        prob = [None] * n_items
+        diag_r = [None] * n_items
+        weights_t = [None] * n_items
+        o_ps = [None] * n_items
+        o_bf = held.tile([P, H, N], BF16, name="o_bf")
+
+        def key_starts(jb):
+            return list(range(0, (jb + 1) * P, BANK))
+
+        def scores(n):
+            jb, h = items[n]
             keys = (jb + 1) * P
-            queries = slice(jb * P, keys)
-            starts = list(range(0, keys, BANK))
-
-            score = []
-            for a in starts:
+            banks = []
+            for a in key_starts(jb):
                 b = min(a + BANK, keys)
                 s_ps = new_bank()
                 past = min(b, jb * P)
                 if past > a:
                     nc.tensor.matmul(
-                        s_ps[:, 0 : past - a],
-                        lhsT=q_bf[h][:, queries],
-                        rhs=k_bf[h][:, a:past],
-                        start=True,
-                        stop=True,
+                        s_ps[:, 0 : past - a], lhsT=q_bf[:, h, block_cols(jb)], rhs=k_bf[:, h, a:past],
+                        start=True, stop=True,
                     )
                 if b == keys:
                     own = s_ps[:, jb * P - a : keys - a]
                     nc.tensor.matmul(
-                        own, lhsT=q_bf[h][:, queries], rhs=k_bf[h][:, queries],
+                        own, lhsT=q_bf[:, h, block_cols(jb)], rhs=k_bf[:, h, block_cols(jb)],
                         start=True, stop=False,
                     )
                     nc.tensor.matmul(own, lhsT=ident[:], rhs=mask[:], start=False, stop=True)
-                score.append(s_ps)
-
-            neg_max_parts = small.tile([P, 2], F32, name="neg_max_parts")
-            for i, a in enumerate(starts):
+                banks.append(s_ps)
+            score_ps[n] = banks
+            parts = small.tile([P, len(banks)], F32, name="neg_max_parts")
+            for i, a in enumerate(key_starts(jb)):
                 nc.vector.tensor_reduce(
-                    out=neg_max_parts[:, i : i + 1],
-                    in_=score[i][:, 0 : min(BANK, keys - a)],
-                    axis=AXIS.X,
-                    op=ALU.max,
-                    negate=True,
+                    out=parts[:, i : i + 1], in_=banks[i][:, 0 : min(BANK, keys - a)],
+                    axis=AXIS.X, op=ALU.max, negate=True,
                 )
-            if len(starts) == 2:
-                neg_max = small.tile([P, 1], F32, name="neg_max")
-                nc.vector.tensor_tensor(
-                    neg_max[:], neg_max_parts[:, 0:1], neg_max_parts[:, 1:2], ALU.min
-                )
+            if len(banks) == 1:
+                neg_max[n] = parts
             else:
-                neg_max = neg_max_parts
+                neg_max[n] = small.tile([P, 1], F32, name="neg_max")
+                nc.vector.tensor_tensor(neg_max[n][:], parts[:, 0:1], parts[:, 1:2], ALU.min)
 
-            prob = ring.tile([P, N], BF16, name="prob")
-            sum_parts = small.tile([P, 2], F32, name="sum_parts")
-            for i, a in enumerate(starts):
+        def exps(n):
+            jb, h = items[n]
+            keys = (jb + 1) * P
+            banks = score_ps[n]
+            prob[n] = ring.tile([P, N], BF16, name="prob")
+            parts = small.tile([P, len(banks)], F32, name="sum_parts")
+            for i, a in enumerate(key_starts(jb)):
                 b = min(a + BANK, keys)
                 nc.scalar.activation(
-                    out=prob[:, a:b],
-                    in_=score[i][:, 0 : b - a],
-                    func=ACT.Exp,
-                    bias=neg_max[:, 0:1],
-                    scale=1.0,
-                    accum_out=sum_parts[:, i : i + 1],
+                    out=prob[n][:, a:b], in_=banks[i][:, 0 : b - a], func=ACT.Exp,
+                    bias=neg_max[n][:, 0:1], scale=1.0, accum_out=parts[:, i : i + 1],
                 )
-            if len(starts) == 2:
-                total = small.tile([P, 1], F32, name="total")
-                nc.vector.tensor_tensor(total[:], sum_parts[:, 0:1], sum_parts[:, 1:2], ALU.add)
+            if len(banks) == 1:
+                total = parts
             else:
-                total = sum_parts
+                total = small.tile([P, 1], F32, name="total")
+                nc.vector.tensor_tensor(total[:], parts[:, 0:1], parts[:, 1:2], ALU.add)
             recip = small.tile([P, 1], F32, name="recip")
             nc.vector.reciprocal(recip[:], total[:, 0:1])
-
-            diag_r = ring.tile([P, P], BF16, name="diag_r")
-            nc.gpsimd.tensor_scalar(
-                out=diag_r[:], in0=ident[:], scalar1=recip[:, 0:1], scalar2=0.0,
-                op0=ALU.mult, op1=ALU.add,
+            diag_r[n] = ring.tile([P, P], BF16, name="diag_r")
+            nc.vector.tensor_scalar(
+                out=diag_r[n][:], in0=ident[:], scalar1=recip[:, 0:1], scalar2=None, op0=ALU.mult
             )
-            weights_t = ring.tile([P, N], BF16, name="weights_t")
-            for a in starts:
-                b = min(a + BANK, keys)
-                t_ps = new_bank()
-                for tb in range(a // P, b // P):
-                    nc.tensor.matmul(
-                        t_ps[:, tb * P - a : (tb + 1) * P - a],
-                        lhsT=prob[:, tb * P : (tb + 1) * P],
-                        rhs=diag_r[:],
-                        start=True,
-                        stop=True,
-                    )
-                if h % 2 == 0:
-                    nc.vector.tensor_copy(weights_t[:, a:b], t_ps[:, 0 : b - a])
-                else:
-                    nc.scalar.copy(weights_t[:, a:b], t_ps[:, 0 : b - a])
 
-            o_ps = new_bank()
+        def flip(n):
+            jb, h = items[n]
+            keys = (jb + 1) * P
+            t_ps = new_bank(BF16, 2 * BANK)
             for tb in range(jb + 1):
                 nc.tensor.matmul(
-                    o_ps[:, 0:P],
-                    lhsT=v_t[tb][:, h * P : (h + 1) * P],
-                    rhs=weights_t[:, tb * P : (tb + 1) * P],
-                    start=(tb == 0),
-                    stop=(tb == jb),
+                    t_ps[:, block_cols(tb)], lhsT=prob[n][:, block_cols(tb)], rhs=diag_r[n][:],
+                    start=True, stop=True,
                 )
+            weights_t[n] = ring.tile([P, N], BF16, name="weights_t")
+            nc.vector.tensor_copy(weights_t[n][:, 0:keys], t_ps[:, 0:keys])
+
+        def mix(n):
+            jb, h = items[n]
+            o_ps[n] = new_bank()
+            for tb in range(jb + 1):
+                nc.tensor.matmul(
+                    o_ps[n][:, 0:P], lhsT=v_t[tb][:, block_cols(h)], rhs=weights_t[n][:, block_cols(tb)],
+                    start=(tb == 0), stop=(tb == jb),
+                )
+
+        def store_o(n):
+            jb, h = items[n]
             nc.scalar.activation(
-                out=o_bf[h][:, queries], in_=o_ps[:, 0:P], func=ACT.Identity,
+                out=o_bf[:, h, block_cols(jb)], in_=o_ps[n][:, 0:P], func=ACT.Identity,
                 bias=bv_sb[:, h : h + 1], scale=1.0,
             )
 
-        def finish(half):
-            cols = slice(half * BANK, (half + 1) * BANK)
-            y, y_bf = [], []
+        y = [None] * TB
+        y_sq = [None] * TB
+        rstd = [None] * TB
+
+        def project_y(tb):
+            y_ps = new_bank()
             for eb in range(CB):
-                y_ps = new_bank()
                 for c in range(CB):
                     nc.tensor.matmul(
-                        y_ps[:],
-                        lhsT=wo_sb[:, c, eb * P : (eb + 1) * P],
-                        rhs=o_bf[c][:, cols],
-                        start=(c == 0),
-                        stop=(c == CB - 1),
+                        y_ps[:, block_cols(eb)], lhsT=wo_centred[:, c, block_cols(eb)], rhs=o_bf[:, c, block_cols(tb)],
+                        start=(c == 0), stop=(c == CB - 1),
                     )
-                y_eb = norm.tile([P, BANK], F32, name=f"y{eb}")
-                nc.vector.scalar_tensor_tensor(
-                    out=y_eb[:], in0=y_ps[:], scalar=bo_sb[:, eb : eb + 1], in1=x[eb][:, cols],
-                    op0=ALU.add, op1=ALU.add,
-                )
-                y.append(y_eb)
-                y_bf_eb = norm.tile([P, BANK], BF16, name=f"y_bf{eb}")
-                nc.gpsimd.tensor_scalar(
-                    out=y_bf_eb[:], in0=y_eb[:], scalar1=1.0, scalar2=0.0,
-                    op0=ALU.mult, op1=ALU.add,
-                )
-                y_bf.append(y_bf_eb)
-            mean_ps = new_bank()
-            for eb in range(CB):
-                nc.tensor.matmul(
-                    mean_ps[:], lhsT=averager[:], rhs=y_bf[eb][:],
-                    start=(eb == 0), stop=(eb == CB - 1),
-                )
+            y[tb] = norm.tile([P, CB, P], F32, name="y")
+            nc.vector.tensor_tensor(
+                y[tb][:], y_ps[:].rearrange("p (a t) -> p a t", t=P), x[:, :, block_cols(tb)], ALU.add
+            )
+            y_sq[tb] = norm.tile([P, CB, P], BF16, name="y_sq")
+            nc.gpsimd.tensor_tensor(y_sq[tb][:], y[tb][:], y[tb][:], ALU.mult)
+
+        def deviation(tb):
             var_ps = new_bank()
             for eb in range(CB):
-                nc.vector.tensor_tensor(y[eb][:], y[eb][:], mean_ps[:], ALU.subtract)
-                sq_eb = norm.tile([P, BANK], BF16, name=f"sq{eb}")
-                nc.gpsimd.tensor_tensor(sq_eb[:], y[eb][:], y[eb][:], ALU.mult)
                 nc.tensor.matmul(
-                    var_ps[:], lhsT=averager[:], rhs=sq_eb[:],
+                    var_ps[:, 0:P], lhsT=averager[:], rhs=y_sq[tb][:, eb, :],
                     start=(eb == 0), stop=(eb == CB - 1),
                 )
-            rstd = norm.tile([P, BANK], F32, name="rstd")
+            log_var = norm.tile([P, P], F32, name="log_var")
             nc.scalar.activation(
-                out=rstd[:], in_=var_ps[:], func=ACT.Abs_reciprocal_sqrt,
-                bias=eps_col[:, 0:1], scale=1.0,
+                out=log_var[:], in_=var_ps[:, 0:P], func=ACT.Ln, bias=eps_col[:, 0:1], scale=1.0
+            )
+            rstd[tb] = norm.tile([P, P], F32, name="rstd")
+            nc.scalar.activation(out=rstd[tb][:], in_=log_var[:], func=ACT.Exp, scale=-0.5)
+
+        def normalise(tb):
+            nc.vector.tensor_tensor(
+                y[tb][:], y[tb][:], rstd[tb][:].unsqueeze(1).to_broadcast([P, CB, P]), ALU.mult
             )
             for eb in range(CB):
-                nc.vector.scalar_tensor_tensor(
-                    out=y[eb][:], in0=y[eb][:], scalar=gain_sb[:, eb : eb + 1], in1=rstd[:],
-                    op0=ALU.mult, op1=ALU.mult,
-                )
                 nc.gpsimd.tensor_scalar(
-                    out=y[eb][:], in0=y[eb][:], scalar1=1.0, scalar2=shift_sb[:, eb : eb + 1],
+                    out=y[tb][:, eb, :], in0=y[tb][:, eb, :],
+                    scalar1=gain_sb[:, eb : eb + 1], scalar2=shift_sb[:, eb : eb + 1],
                     op0=ALU.mult, op1=ALU.add,
                 )
-                nc.sync.dma_start(out[eb * P : (eb + 1) * P, cols], y[eb][:])
+            nc.sync.dma_start(out.rearrange("(a p) j -> p a j", p=P)[:, :, block_cols(tb)], y[tb][:])
 
-        for jb in range(TB):
-            for h in range(H):
-                attend(jb, h)
-            if (jb + 1) * P % BANK == 0:
-                finish((jb + 1) * P // BANK - 1)
+        for piece in range(3):
+            prepare(0, piece)
+        for n in range(n_items + STORE_LAG + NORMALISE_LAG + 1):
+            if 0 <= n - STORE_LAG < n_items:
+                store_o(n - STORE_LAG)
+            if n < n_items - H:
+                prepare(n // H + 1, n % H)
+            if n < n_items and n % H == H - 1:
+                centre_x(n // H)
+            if n < n_items:
+                scores(n)
+            if 1 <= n <= CB:
+                centre_wo(n - 1)
+            if 0 <= n - EXP_LAG < n_items:
+                exps(n - EXP_LAG)
+            if 0 <= n - FLIP_LAG < n_items:
+                flip(n - FLIP_LAG)
+            if 0 <= n - MIX_LAG < n_items:
+                mix(n - MIX_LAG)
+            since_store = n - STORE_LAG - (H - 1)
+            for lag, stage in ((PROJECT_LAG, project_y), (DEVIATION_LAG, deviation), (NORMALISE_LAG, normalise)):
+                if (since_store - lag) % H == 0 and 0 <= (since_store - lag) // H < TB:
+                    stage((since_store - lag) // H)

@@ -20,7 +20,7 @@ EPS = 1e-5
 MASKED = -1e30
 
 EXP_LAG, FLIP_LAG, MIX_LAG, STORE_LAG = 1, 3, 5, 6
-PROJECT_LAG, DEVIATION_LAG, NORMALISE_LAG = 0, 2, 3
+PROJECT_LAG, DEVIATION_LAG, NORMALISE_LAG, OUT_LAG = 0, 2, 4, 5
 
 FLOPS = 4 * 2 * D * D * N + 2 * 2 * D * (N * (N + 1) // 2)
 
@@ -94,22 +94,14 @@ def tile_sequencedecodermoe_b_kernel(
         nc.gpsimd.memset(averager[:], 1.0 / D)
         averager_f32 = held.tile([P, P], F32, name="averager_f32")
         nc.gpsimd.memset(averager_f32[:], 1.0 / D)
-        eps_col = held.tile([P, 1], F32, name="eps_col")
-        nc.gpsimd.memset(eps_col[:], EPS)
-
-        bo_mean_ps = new_bank()
-        nc.tensor.matmul(bo_mean_ps[:, 0:CB], lhsT=averager_f32[:], rhs=bo_sb[:], start=True, stop=True)
-        bo_mean = small.tile([P, 1], F32, name="bo_mean")
-        nc.vector.tensor_reduce(out=bo_mean[:], in_=bo_mean_ps[:, 0:CB], axis=AXIS.X, op=ALU.add)
-        bo_centred = held.tile([P, CB], F32, name="bo_centred")
-        nc.vector.tensor_scalar(
-            out=bo_centred[:], in0=bo_sb[:], scalar1=bo_mean[:, 0:1], scalar2=None, op0=ALU.subtract
-        )
-
-        bq_scaled = held.tile([P, CB], F32, name="bq_scaled")
-        nc.vector.tensor_scalar(
-            out=bq_scaled[:], in0=bq_sb[:], scalar1=1.0 / math.sqrt(P), scalar2=None, op0=ALU.mult
-        )
+        averager_col = held.tile([P, 1], BF16, name="averager_col")
+        nc.gpsimd.memset(averager_col[:], 1.0 / D)
+        ones_f32 = held.tile([P, P], F32, name="ones_f32")
+        nc.gpsimd.memset(ones_f32[:], 1.0)
+        ident_f32 = held.tile([P, P], F32, name="ident_f32")
+        make_identity(nc, ident_f32[:])
+        neg_half = held.tile([P, 1], F32, name="neg_half")
+        nc.gpsimd.memset(neg_half[:], -0.5)
 
         x = held.tile([P, CB, N], F32, name="x")
         x_bf = held.tile([P, CB, N], BF16, name="x_bf")
@@ -133,25 +125,26 @@ def tile_sequencedecodermoe_b_kernel(
                         stop=(c == CB - 1),
                     )
 
-        for c in range(CB):
-            nc.gpsimd.tensor_scalar(
-                out=x[:, c, :], in0=x[:, c, :], scalar1=1.0, scalar2=bo_centred[:, c : c + 1],
-                op0=ALU.mult, op1=ALU.add,
-            )
-
         q_bf = held.tile([P, H, N], BF16, name="q_bf")
         for h in range(H):
             nc.vector.tensor_scalar(
-                out=q_bf[:, h, half_cols(0)],
-                in0=q_ps[h][0][:],
-                scalar1=bq_sb[:, h : h + 1],
-                scalar2=1.0 / math.sqrt(P),
+                out=q_bf[:, h, half_cols(0)], in0=q_ps[h][0][:], scalar1=bq_sb[:, h : h + 1], scalar2=None,
                 op0=ALU.add,
-                op1=ALU.mult,
             )
             nc.scalar.activation(
                 out=q_bf[:, h, half_cols(1)], in_=q_ps[h][1][:], func=ACT.Identity,
-                bias=bq_scaled[:, h : h + 1], scale=1.0 / math.sqrt(P),
+                bias=bq_sb[:, h : h + 1], scale=1.0,
+            )
+
+        bo_centred = held.tile([P, CB], F32, name="bo_centred")
+
+        def centre_bo():
+            bo_mean_ps = new_bank()
+            nc.tensor.matmul(bo_mean_ps[:, 0:CB], lhsT=averager_f32[:], rhs=bo_sb[:], start=True, stop=True)
+            bo_mean = small.tile([P, 1], F32, name="bo_mean")
+            nc.vector.tensor_reduce(out=bo_mean[:], in_=bo_mean_ps[:, 0:CB], axis=AXIS.X, op=ALU.add)
+            nc.vector.tensor_scalar(
+                out=bo_centred[:], in0=bo_sb[:], scalar1=bo_mean[:, 0:1], scalar2=None, op0=ALU.subtract
             )
 
         wo_centred = held.tile([P, CB, D], BF16, name="wo_centred")
@@ -179,9 +172,10 @@ def tile_sequencedecodermoe_b_kernel(
                         k_ps[:, block_cols(i)], lhsT=wk_sb[:, c, block_cols(h)], rhs=x_bf[:, c, block_cols(tb)],
                         start=(c == 0), stop=(c == CB - 1),
                     )
-            nc.scalar.copy(
+            nc.scalar.mul(
                 k_bf[:, heads[0] : heads[-1] + 1, block_cols(tb)],
                 k_ps[:, 0 : len(heads) * P].rearrange("p (h t) -> p h t", t=P),
+                1.0 / math.sqrt(P),
             )
 
         def project_v(tb):
@@ -200,12 +194,11 @@ def tile_sequencedecodermoe_b_kernel(
                     x_mean_ps[:, 0:P], lhsT=averager[:], rhs=x_bf[:, c, block_cols(tb)],
                     start=(c == 0), stop=(c == CB - 1),
                 )
-            nc.vector.tensor_tensor(
-                x[:, :, block_cols(tb)],
-                x[:, :, block_cols(tb)],
-                x_mean_ps[:, 0:P].unsqueeze(1).to_broadcast([P, CB, P]),
-                ALU.subtract,
-            )
+            for c in range(CB):
+                nc.vector.scalar_tensor_tensor(
+                    out=x[:, c, block_cols(tb)], in0=x[:, c, block_cols(tb)], scalar=bo_centred[:, c : c + 1],
+                    in1=x_mean_ps[:, 0:P], op0=ALU.add, op1=ALU.subtract,
+                )
 
         def prepare(tb, piece):
             if piece == 0:
@@ -316,19 +309,23 @@ def tile_sequencedecodermoe_b_kernel(
 
         y = [None] * TB
         y_sq = [None] * TB
-        rstd = [None] * TB
+        y_ps = [None] * TB
+        diag_rstd = [None] * TB
 
-        def project_y(tb):
-            y_ps = new_bank()
+        def project_y(n):
+            tb, h = items[n]
+            if h == 0:
+                y_ps[tb] = new_bank()
             for eb in range(CB):
-                for c in range(CB):
-                    nc.tensor.matmul(
-                        y_ps[:, block_cols(eb)], lhsT=wo_centred[:, c, block_cols(eb)], rhs=o_bf[:, c, block_cols(tb)],
-                        start=(c == 0), stop=(c == CB - 1),
-                    )
+                nc.tensor.matmul(
+                    y_ps[tb][:, block_cols(eb)], lhsT=wo_centred[:, h, block_cols(eb)], rhs=o_bf[:, h, block_cols(tb)],
+                    start=(h == 0 and eb == 0), stop=(h == H - 1 and eb == CB - 1),
+                )
+
+        def residual(tb):
             y[tb] = norm.tile([P, CB, P], F32, name="y")
             nc.vector.tensor_tensor(
-                y[tb][:], y_ps[:].rearrange("p (a t) -> p a t", t=P), x[:, :, block_cols(tb)], ALU.add
+                y[tb][:], y_ps[tb][:].rearrange("p (a t) -> p a t", t=P), x[:, :, block_cols(tb)], ALU.add
             )
             y_sq[tb] = norm.tile([P, CB, P], BF16, name="y_sq")
             nc.gpsimd.tensor_tensor(y_sq[tb][:], y[tb][:], y[tb][:], ALU.mult)
@@ -337,31 +334,43 @@ def tile_sequencedecodermoe_b_kernel(
             var_ps = new_bank()
             for eb in range(CB):
                 nc.tensor.matmul(
-                    var_ps[:, 0:P], lhsT=averager[:], rhs=y_sq[tb][:, eb, :],
+                    var_ps[:, 0:1], lhsT=y_sq[tb][:, eb, :], rhs=averager_col[:],
                     start=(eb == 0), stop=(eb == CB - 1),
                 )
-            log_var = norm.tile([P, P], F32, name="log_var")
-            nc.scalar.activation(
-                out=log_var[:], in_=var_ps[:, 0:P], func=ACT.Ln, bias=eps_col[:, 0:1], scale=1.0
+            var_eps = small.tile([P, 1], F32, name="var_eps")
+            nc.vector.tensor_scalar(
+                out=var_eps[:], in0=var_ps[:, 0:1], scalar1=EPS, scalar2=None, op0=ALU.add
             )
-            rstd[tb] = norm.tile([P, P], F32, name="rstd")
-            nc.scalar.activation(out=rstd[tb][:], in_=log_var[:], func=ACT.Exp, scale=-0.5)
+            rstd = small.tile([P, 1], F32, name="rstd")
+            nc.gpsimd.tensor_tensor(rstd[:], var_eps[:], neg_half[:], ALU.pow)
+            diag_rstd[tb] = norm.tile([P, P], F32, name="diag_rstd")
+            nc.gpsimd.tensor_scalar(
+                out=diag_rstd[tb][:], in0=ident_f32[:], scalar1=rstd[:, 0:1], scalar2=0.0,
+                op0=ALU.mult, op1=ALU.add,
+            )
 
         def normalise(tb):
+            rstd_ps = new_bank()
+            nc.tensor.matmul(rstd_ps[:, 0:P], lhsT=ones_f32[:], rhs=diag_rstd[tb][:], start=True, stop=True)
             nc.vector.tensor_tensor(
-                y[tb][:], y[tb][:], rstd[tb][:].unsqueeze(1).to_broadcast([P, CB, P]), ALU.mult
+                y[tb][:], y[tb][:], rstd_ps[:, 0:P].unsqueeze(1).to_broadcast([P, CB, P]), ALU.mult
             )
+
+        def store_y(tb):
             for eb in range(CB):
-                nc.gpsimd.tensor_scalar(
-                    out=y[tb][:, eb, :], in0=y[tb][:, eb, :],
-                    scalar1=gain_sb[:, eb : eb + 1], scalar2=shift_sb[:, eb : eb + 1],
-                    op0=ALU.mult, op1=ALU.add,
+                nc.scalar.activation(
+                    out=y[tb][:, eb, :], in_=y[tb][:, eb, :], func=ACT.Identity,
+                    bias=shift_sb[:, eb : eb + 1], scale=gain_sb[:, eb : eb + 1],
                 )
             nc.sync.dma_start(out.rearrange("(a p) j -> p a j", p=P)[:, :, block_cols(tb)], y[tb][:])
 
         for piece in range(3):
             prepare(0, piece)
-        for n in range(n_items + STORE_LAG + NORMALISE_LAG + 1):
+        def block_due(n, lag):
+            steps = n - lag - STORE_LAG - (H - 1)
+            return steps // H if steps % H == 0 and 0 <= steps // H < TB else None
+
+        for n in range(n_items + STORE_LAG + OUT_LAG + 1):
             if 0 <= n - STORE_LAG < n_items:
                 store_o(n - STORE_LAG)
             if n < n_items - H:
@@ -370,6 +379,8 @@ def tile_sequencedecodermoe_b_kernel(
                 centre_x(n // H)
             if n < n_items:
                 scores(n)
+            if n == 0:
+                centre_bo()
             if 1 <= n <= CB:
                 centre_wo(n - 1)
             if 0 <= n - EXP_LAG < n_items:
@@ -378,7 +389,13 @@ def tile_sequencedecodermoe_b_kernel(
                 flip(n - FLIP_LAG)
             if 0 <= n - MIX_LAG < n_items:
                 mix(n - MIX_LAG)
-            since_store = n - STORE_LAG - (H - 1)
-            for lag, stage in ((PROJECT_LAG, project_y), (DEVIATION_LAG, deviation), (NORMALISE_LAG, normalise)):
-                if (since_store - lag) % H == 0 and 0 <= (since_store - lag) // H < TB:
-                    stage((since_store - lag) // H)
+            if 0 <= n - STORE_LAG < n_items:
+                project_y(n - STORE_LAG)
+            if block_due(n, PROJECT_LAG) is not None:
+                residual(block_due(n, PROJECT_LAG))
+            if block_due(n, DEVIATION_LAG) is not None:
+                deviation(block_due(n, DEVIATION_LAG))
+            if block_due(n, NORMALISE_LAG) is not None:
+                normalise(block_due(n, NORMALISE_LAG))
+            if block_due(n, OUT_LAG) is not None:
+                store_y(block_due(n, OUT_LAG))

@@ -17,6 +17,7 @@ TB = N // P
 BANK = 512
 HALVES = N // BANK
 EPS = 1e-5
+PIECE = 256
 MASKED = -1e30
 
 EXP_LAG, FLIP_LAG, MIX_LAG, STORE_LAG = 1, 3, 5, 6
@@ -103,27 +104,37 @@ def tile_sequencedecodermoe_b_kernel(
         neg_half = held.tile([P, 1], F32, name="neg_half")
         nc.gpsimd.memset(neg_half[:], -0.5)
 
+        exp_warm_up = held.tile([P, 1], F32, name="exp_warm_up")
+        nc.vector.memset(exp_warm_up[:], 0.0)
+        nc.scalar.activation(out=exp_warm_up[:], in_=exp_warm_up[:], func=ACT.Exp)
+
         x = held.tile([P, CB, N], F32, name="x")
         x_bf = held.tile([P, CB, N], BF16, name="x_bf")
         q_ps = [[new_bank() for half in range(HALVES)] for h in range(H)]
         for c in range(CB):
-            for half in range(HALVES):
-                cols = half_cols(half)
+            for piece in range(N // PIECE):
+                cols = slice(piece * PIECE, (piece + 1) * PIECE)
                 nc.vector.tensor_tensor(
                     x[:, c, cols],
-                    emb_sb[c][:].indirect(offsets[:, half * (BANK // 16) : (half + 1) * (BANK // 16)]),
+                    emb_sb[c][:].indirect(offsets[:, piece * (PIECE // 16) : (piece + 1) * (PIECE // 16)]),
                     pos_sb[c][:, cols],
                     ALU.add,
                 )
                 nc.scalar.copy(x_bf[:, c, cols], x[:, c, cols])
                 for h in range(H):
                     nc.tensor.matmul(
-                        q_ps[h][half][:],
+                        q_ps[h][piece * PIECE // BANK][:, piece * PIECE % BANK : piece * PIECE % BANK + PIECE],
                         lhsT=wq_sb[:, c, block_cols(h)],
                         rhs=x_bf[:, c, cols],
-                        start=(c == 0),
-                        stop=(c == CB - 1),
+                        start=(c == 0 and piece * PIECE % BANK == 0),
+                        stop=(c == CB - 1 and (piece + 1) * PIECE % BANK == 0),
                     )
+
+        x_pair_sum = held.tile([P, 2, N], F32, name="x_pair_sum")
+        x_blocks_sum = held.tile([P, N], BF16, name="x_blocks_sum")
+        nc.gpsimd.tensor_tensor(x_pair_sum[:, 0, :], x[:, 3, :], x[:, 0, :], ALU.add)
+        nc.gpsimd.tensor_tensor(x_pair_sum[:, 1, :], x[:, 1, :], x[:, 2, :], ALU.add)
+        nc.gpsimd.tensor_tensor(x_blocks_sum[:], x_pair_sum[:, 0, :], x_pair_sum[:, 1, :], ALU.add)
 
         q_bf = held.tile([P, H, N], BF16, name="q_bf")
         for h in range(H):
@@ -189,11 +200,9 @@ def tile_sequencedecodermoe_b_kernel(
 
         def centre_x(tb):
             x_mean_ps = new_bank()
-            for c in range(CB):
-                nc.tensor.matmul(
-                    x_mean_ps[:, 0:P], lhsT=averager[:], rhs=x_bf[:, c, block_cols(tb)],
-                    start=(c == 0), stop=(c == CB - 1),
-                )
+            nc.tensor.matmul(
+                x_mean_ps[:, 0:P], lhsT=averager[:], rhs=x_blocks_sum[:, block_cols(tb)], start=True, stop=True
+            )
             for c in range(CB):
                 nc.vector.scalar_tensor_tensor(
                     out=x[:, c, block_cols(tb)], in0=x[:, c, block_cols(tb)], scalar=bo_centred[:, c : c + 1],
@@ -253,7 +262,7 @@ def tile_sequencedecodermoe_b_kernel(
                 neg_max[n] = parts
             else:
                 neg_max[n] = small.tile([P, 1], F32, name="neg_max")
-                nc.vector.tensor_tensor(neg_max[n][:], parts[:, 0:1], parts[:, 1:2], ALU.min)
+                nc.vector.tensor_reduce(out=neg_max[n][:], in_=parts[:], axis=AXIS.X, op=ALU.min)
 
         def exps(n):
             jb, h = items[n]
@@ -271,13 +280,11 @@ def tile_sequencedecodermoe_b_kernel(
                 total = parts
             else:
                 total = small.tile([P, 1], F32, name="total")
-                nc.vector.tensor_tensor(total[:], parts[:, 0:1], parts[:, 1:2], ALU.add)
+                nc.vector.tensor_reduce(out=total[:], in_=parts[:], axis=AXIS.X, op=ALU.add)
             recip = small.tile([P, 1], F32, name="recip")
             nc.vector.reciprocal(recip[:], total[:, 0:1])
             diag_r[n] = ring.tile([P, P], BF16, name="diag_r")
-            nc.vector.tensor_scalar(
-                out=diag_r[n][:], in0=ident[:], scalar1=recip[:, 0:1], scalar2=None, op0=ALU.mult
-            )
+            nc.scalar.activation(out=diag_r[n][:], in_=ident[:], func=ACT.Identity, scale=recip[:, 0:1])
 
         def flip(n):
             jb, h = items[n]
@@ -310,7 +317,7 @@ def tile_sequencedecodermoe_b_kernel(
         y = [None] * TB
         y_sq = [None] * TB
         y_ps = [None] * TB
-        diag_rstd = [None] * TB
+        rstd_rows = [None] * TB
 
         def project_y(n):
             tb, h = items[n]
@@ -328,7 +335,8 @@ def tile_sequencedecodermoe_b_kernel(
                 y[tb][:], y_ps[tb][:].rearrange("p (a t) -> p a t", t=P), x[:, :, block_cols(tb)], ALU.add
             )
             y_sq[tb] = norm.tile([P, CB, P], BF16, name="y_sq")
-            nc.gpsimd.tensor_tensor(y_sq[tb][:], y[tb][:], y[tb][:], ALU.mult)
+            squarer = nc.vector if tb == TB - 1 else nc.gpsimd
+            squarer.tensor_tensor(y_sq[tb][:], y[tb][:], y[tb][:], ALU.mult)
 
         def deviation(tb):
             var_ps = new_bank()
@@ -343,15 +351,15 @@ def tile_sequencedecodermoe_b_kernel(
             )
             rstd = small.tile([P, 1], F32, name="rstd")
             nc.gpsimd.tensor_tensor(rstd[:], var_eps[:], neg_half[:], ALU.pow)
-            diag_rstd[tb] = norm.tile([P, P], F32, name="diag_rstd")
+            rstd_rows[tb] = norm.tile([P, P], F32, name="rstd_rows")
             nc.gpsimd.tensor_scalar(
-                out=diag_rstd[tb][:], in0=ident_f32[:], scalar1=rstd[:, 0:1], scalar2=0.0,
+                out=rstd_rows[tb][:], in0=ones_f32[:], scalar1=rstd[:, 0:1], scalar2=0.0,
                 op0=ALU.mult, op1=ALU.add,
             )
 
         def normalise(tb):
             rstd_ps = new_bank()
-            nc.tensor.matmul(rstd_ps[:, 0:P], lhsT=ones_f32[:], rhs=diag_rstd[tb][:], start=True, stop=True)
+            nc.tensor.transpose(rstd_ps[:, 0:P], rstd_rows[tb][:], ident_f32[:])
             nc.vector.tensor_tensor(
                 y[tb][:], y[tb][:], rstd_ps[:, 0:P].unsqueeze(1).to_broadcast([P, CB, P]), ALU.mult
             )
@@ -375,8 +383,8 @@ def tile_sequencedecodermoe_b_kernel(
                 store_o(n - STORE_LAG)
             if n < n_items - H:
                 prepare(n // H + 1, n % H)
-            if n < n_items and n % H == H - 1:
-                centre_x(n // H)
+            if H <= n < n_items + H and n % H == H - 1:
+                centre_x(n // H - 1)
             if n < n_items:
                 scores(n)
             if n == 0:

@@ -15,13 +15,13 @@ D, V, N, H = 512, 2048, 1024, 4
 CB = D // P
 TB = N // P
 BANK = 512
-HALVES = N // BANK
-EPS = 1e-5
+PSUM_BANKS = 8
 PIECE = 256
+EPS = 1e-5
 MASKED = -1e30
 
 EXP_LAG, FLIP_LAG, MIX_LAG, STORE_LAG = 1, 3, 5, 6
-PROJECT_LAG, DEVIATION_LAG, NORMALISE_LAG, OUT_LAG = 0, 2, 4, 5
+RESIDUAL_LAG, DEVIATION_LAG, NORMALISE_LAG, OUT_LAG = 0, 2, 4, 6
 
 FLOPS = 4 * 2 * D * D * N + 2 * 2 * D * (N * (N + 1) // 2)
 
@@ -32,19 +32,16 @@ def tile_sequencedecodermoe_b_kernel(
     nc = tc.nc
     with (
         tc.tile_pool(name="held", bufs=1) as held,
-        tc.tile_pool(name="ring", bufs=6) as ring,
-        tc.tile_pool(name="small", bufs=8) as small,
+        tc.tile_pool(name="ring", bufs=MIX_LAG + 1) as ring,
+        tc.tile_pool(name="small", bufs=MIX_LAG + 1) as small,
         tc.tile_pool(name="norm", bufs=3) as norm,
-        tc.psum_pool(name="psum", bufs=8) as psum,
+        tc.psum_pool(name="psum", bufs=PSUM_BANKS) as psum,
     ):
 
         def new_bank(dtype=F32, cols=BANK):
             return psum.tile([P, cols], dtype, name="bank", tag="bank")
 
-        def half_cols(half):
-            return slice(half * BANK, (half + 1) * BANK)
-
-        def block_cols(b):
+        def block(b):
             return slice(b * P, (b + 1) * P)
 
         offsets = held.tile([P, N // 16], U16, name="offsets")
@@ -58,8 +55,8 @@ def tile_sequencedecodermoe_b_kernel(
         emb_sb = [held.tile([P, V], F32, name=f"emb{c}") for c in range(CB)]
         pos_sb = [held.tile([P, N], F32, name=f"pos{c}") for c in range(CB)]
         for c in range(CB):
-            nc.sync.dma_start(emb_sb[c][:], emb[block_cols(c), :])
-            nc.scalar.dma_start(pos_sb[c][:], pos[block_cols(c), :])
+            nc.sync.dma_start(emb_sb[c][:], emb[block(c), :])
+            nc.scalar.dma_start(pos_sb[c][:], pos[block(c), :])
             if c == 1:
                 wq_sb = load_weight(wq, "wq_sb", nc.scalar)
         wk_sb = load_weight(wk, "wk_sb", nc.sync)
@@ -110,44 +107,45 @@ def tile_sequencedecodermoe_b_kernel(
 
         x = held.tile([P, CB, N], F32, name="x")
         x_bf = held.tile([P, CB, N], BF16, name="x_bf")
-        q_ps = [[new_bank() for half in range(HALVES)] for h in range(H)]
+        q_ps = [[new_bank() for half in range(N // BANK)] for h in range(H)]
         for c in range(CB):
-            for piece in range(N // PIECE):
-                cols = slice(piece * PIECE, (piece + 1) * PIECE)
+            for first in range(0, N, PIECE):
+                tokens = slice(first, first + PIECE)
                 nc.vector.tensor_tensor(
-                    x[:, c, cols],
-                    emb_sb[c][:].indirect(offsets[:, piece * (PIECE // 16) : (piece + 1) * (PIECE // 16)]),
-                    pos_sb[c][:, cols],
+                    x[:, c, tokens],
+                    emb_sb[c][:].indirect(offsets[:, first // 16 : (first + PIECE) // 16]),
+                    pos_sb[c][:, tokens],
                     ALU.add,
                 )
-                nc.scalar.copy(x_bf[:, c, cols], x[:, c, cols])
+                nc.scalar.copy(x_bf[:, c, tokens], x[:, c, tokens])
                 for h in range(H):
                     nc.tensor.matmul(
-                        q_ps[h][piece * PIECE // BANK][:, piece * PIECE % BANK : piece * PIECE % BANK + PIECE],
-                        lhsT=wq_sb[:, c, block_cols(h)],
-                        rhs=x_bf[:, c, cols],
-                        start=(c == 0 and piece * PIECE % BANK == 0),
-                        stop=(c == CB - 1 and (piece + 1) * PIECE % BANK == 0),
+                        q_ps[h][first // BANK][:, first % BANK : first % BANK + PIECE],
+                        lhsT=wq_sb[:, c, block(h)],
+                        rhs=x_bf[:, c, tokens],
+                        start=(c == 0 and first % BANK == 0),
+                        stop=(c == CB - 1 and (first + PIECE) % BANK == 0),
                     )
 
         x_pair_sum = held.tile([P, 2, N], F32, name="x_pair_sum")
         x_blocks_sum = held.tile([P, N], BF16, name="x_blocks_sum")
-        nc.gpsimd.tensor_tensor(x_pair_sum[:, 0, :], x[:, 3, :], x[:, 0, :], ALU.add)
+        nc.gpsimd.tensor_tensor(x_pair_sum[:, 0, :], x[:, CB - 1, :], x[:, 0, :], ALU.add)
         nc.gpsimd.tensor_tensor(x_pair_sum[:, 1, :], x[:, 1, :], x[:, 2, :], ALU.add)
         nc.gpsimd.tensor_tensor(x_blocks_sum[:], x_pair_sum[:, 0, :], x_pair_sum[:, 1, :], ALU.add)
 
         q_bf = held.tile([P, H, N], BF16, name="q_bf")
         for h in range(H):
             nc.vector.tensor_scalar(
-                out=q_bf[:, h, half_cols(0)], in0=q_ps[h][0][:], scalar1=bq_sb[:, h : h + 1], scalar2=None,
+                out=q_bf[:, h, 0:BANK], in0=q_ps[h][0][:], scalar1=bq_sb[:, h : h + 1], scalar2=None,
                 op0=ALU.add,
             )
             nc.scalar.activation(
-                out=q_bf[:, h, half_cols(1)], in_=q_ps[h][1][:], func=ACT.Identity,
+                out=q_bf[:, h, BANK:N], in_=q_ps[h][1][:], func=ACT.Identity,
                 bias=bq_sb[:, h : h + 1], scale=1.0,
             )
 
         bo_centred = held.tile([P, CB], F32, name="bo_centred")
+        wo_centred = held.tile([P, CB, D], BF16, name="wo_centred")
 
         def centre_bo():
             bo_mean_ps = new_bank()
@@ -157,8 +155,6 @@ def tile_sequencedecodermoe_b_kernel(
             nc.vector.tensor_scalar(
                 out=bo_centred[:], in0=bo_sb[:], scalar1=bo_mean[:, 0:1], scalar2=None, op0=ALU.subtract
             )
-
-        wo_centred = held.tile([P, CB, D], BF16, name="wo_centred")
 
         def centre_wo(c):
             row_sum = small.tile([P, 1], F32, name="wo_row_sum")
@@ -172,6 +168,17 @@ def tile_sequencedecodermoe_b_kernel(
                 scalar1=1.0, scalar2=neg_mean[:, 0:1], op0=ALU.mult, op1=ALU.add,
             )
 
+        def centre_x(tb):
+            x_mean_ps = new_bank()
+            nc.tensor.matmul(
+                x_mean_ps[:, 0:P], lhsT=averager[:], rhs=x_blocks_sum[:, block(tb)], start=True, stop=True
+            )
+            for c in range(CB):
+                nc.vector.scalar_tensor_tensor(
+                    out=x[:, c, block(tb)], in0=x[:, c, block(tb)], scalar=bo_centred[:, c : c + 1],
+                    in1=x_mean_ps[:, 0:P], op0=ALU.add, op1=ALU.subtract,
+                )
+
         k_bf = held.tile([P, H, N], BF16, name="k_bf")
         v_t = [held.tile([P, D], BF16, name=f"v_t{tb}") for tb in range(TB)]
 
@@ -180,11 +187,11 @@ def tile_sequencedecodermoe_b_kernel(
             for i, h in enumerate(heads):
                 for c in range(CB):
                     nc.tensor.matmul(
-                        k_ps[:, block_cols(i)], lhsT=wk_sb[:, c, block_cols(h)], rhs=x_bf[:, c, block_cols(tb)],
+                        k_ps[:, block(i)], lhsT=wk_sb[:, c, block(h)], rhs=x_bf[:, c, block(tb)],
                         start=(c == 0), stop=(c == CB - 1),
                     )
             nc.scalar.mul(
-                k_bf[:, heads[0] : heads[-1] + 1, block_cols(tb)],
+                k_bf[:, heads[0] : heads[-1] + 1, block(tb)],
                 k_ps[:, 0 : len(heads) * P].rearrange("p (h t) -> p h t", t=P),
                 1.0 / math.sqrt(P),
             )
@@ -193,29 +200,20 @@ def tile_sequencedecodermoe_b_kernel(
             v_ps = new_bank()
             for c in range(CB):
                 nc.tensor.matmul(
-                    v_ps[:], lhsT=x_bf[:, c, block_cols(tb)], rhs=wv_sb[:, c, :],
+                    v_ps[:], lhsT=x_bf[:, c, block(tb)], rhs=wv_sb[:, c, :],
                     start=(c == 0), stop=(c == CB - 1),
                 )
             nc.scalar.copy(v_t[tb][:], v_ps[:])
-
-        def centre_x(tb):
-            x_mean_ps = new_bank()
-            nc.tensor.matmul(
-                x_mean_ps[:, 0:P], lhsT=averager[:], rhs=x_blocks_sum[:, block_cols(tb)], start=True, stop=True
-            )
-            for c in range(CB):
-                nc.vector.scalar_tensor_tensor(
-                    out=x[:, c, block_cols(tb)], in0=x[:, c, block_cols(tb)], scalar=bo_centred[:, c : c + 1],
-                    in1=x_mean_ps[:, 0:P], op0=ALU.add, op1=ALU.subtract,
-                )
 
         def prepare(tb, piece):
             if piece == 0:
                 project_k(tb, [0, 1])
             elif piece == 1:
                 project_k(tb, [2, 3])
-            elif piece == 2:
+            else:
                 project_v(tb)
+
+        prepare_pieces = 3
 
         items = [(jb, h) for jb in range(TB) for h in range(H)]
         n_items = len(items)
@@ -240,14 +238,13 @@ def tile_sequencedecodermoe_b_kernel(
                 past = min(b, jb * P)
                 if past > a:
                     nc.tensor.matmul(
-                        s_ps[:, 0 : past - a], lhsT=q_bf[:, h, block_cols(jb)], rhs=k_bf[:, h, a:past],
+                        s_ps[:, 0 : past - a], lhsT=q_bf[:, h, block(jb)], rhs=k_bf[:, h, a:past],
                         start=True, stop=True,
                     )
                 if b == keys:
                     own = s_ps[:, jb * P - a : keys - a]
                     nc.tensor.matmul(
-                        own, lhsT=q_bf[:, h, block_cols(jb)], rhs=k_bf[:, h, block_cols(jb)],
-                        start=True, stop=False,
+                        own, lhsT=q_bf[:, h, block(jb)], rhs=k_bf[:, h, block(jb)], start=True, stop=False
                     )
                     nc.tensor.matmul(own, lhsT=ident[:], rhs=mask[:], start=False, stop=True)
                 banks.append(s_ps)
@@ -264,7 +261,7 @@ def tile_sequencedecodermoe_b_kernel(
                 neg_max[n] = small.tile([P, 1], F32, name="neg_max")
                 nc.vector.tensor_reduce(out=neg_max[n][:], in_=parts[:], axis=AXIS.X, op=ALU.min)
 
-        def exps(n):
+        def exponentials(n):
             jb, h = items[n]
             keys = (jb + 1) * P
             banks = score_ps[n]
@@ -280,7 +277,9 @@ def tile_sequencedecodermoe_b_kernel(
                 total = parts
             else:
                 total = small.tile([P, 1], F32, name="total")
-                nc.vector.tensor_reduce(out=total[:], in_=parts[:], axis=AXIS.X, op=ALU.add)
+                nc.scalar.activation(
+                    out=total[:], in_=parts[:, 0:1], func=ACT.Identity, bias=parts[:, 1:2], scale=1.0
+                )
             recip = small.tile([P, 1], F32, name="recip")
             nc.vector.reciprocal(recip[:], total[:, 0:1])
             diag_r[n] = ring.tile([P, P], BF16, name="diag_r")
@@ -292,31 +291,33 @@ def tile_sequencedecodermoe_b_kernel(
             t_ps = new_bank(BF16, 2 * BANK)
             for tb in range(jb + 1):
                 nc.tensor.matmul(
-                    t_ps[:, block_cols(tb)], lhsT=prob[n][:, block_cols(tb)], rhs=diag_r[n][:],
-                    start=True, stop=True,
+                    t_ps[:, block(tb)], lhsT=prob[n][:, block(tb)], rhs=diag_r[n][:], start=True, stop=True
                 )
             weights_t[n] = ring.tile([P, N], BF16, name="weights_t")
-            nc.vector.tensor_copy(weights_t[n][:, 0:keys], t_ps[:, 0:keys])
+            if h < H - 1:
+                nc.vector.tensor_copy(weights_t[n][:, 0:keys], t_ps[:, 0:keys])
+            else:
+                nc.scalar.copy(weights_t[n][:, 0:keys], t_ps[:, 0:keys])
 
         def mix(n):
             jb, h = items[n]
             o_ps[n] = new_bank()
             for tb in range(jb + 1):
                 nc.tensor.matmul(
-                    o_ps[n][:, 0:P], lhsT=v_t[tb][:, block_cols(h)], rhs=weights_t[n][:, block_cols(tb)],
+                    o_ps[n][:, 0:P], lhsT=v_t[tb][:, block(h)], rhs=weights_t[n][:, block(tb)],
                     start=(tb == 0), stop=(tb == jb),
                 )
 
         def store_o(n):
             jb, h = items[n]
             nc.scalar.activation(
-                out=o_bf[:, h, block_cols(jb)], in_=o_ps[n][:, 0:P], func=ACT.Identity,
+                out=o_bf[:, h, block(jb)], in_=o_ps[n][:, 0:P], func=ACT.Identity,
                 bias=bv_sb[:, h : h + 1], scale=1.0,
             )
 
+        y_ps = [None] * TB
         y = [None] * TB
         y_sq = [None] * TB
-        y_ps = [None] * TB
         rstd_rows = [None] * TB
 
         def project_y(n):
@@ -325,14 +326,14 @@ def tile_sequencedecodermoe_b_kernel(
                 y_ps[tb] = new_bank()
             for eb in range(CB):
                 nc.tensor.matmul(
-                    y_ps[tb][:, block_cols(eb)], lhsT=wo_centred[:, h, block_cols(eb)], rhs=o_bf[:, h, block_cols(tb)],
+                    y_ps[tb][:, block(eb)], lhsT=wo_centred[:, h, block(eb)], rhs=o_bf[:, h, block(tb)],
                     start=(h == 0 and eb == 0), stop=(h == H - 1 and eb == CB - 1),
                 )
 
         def residual(tb):
             y[tb] = norm.tile([P, CB, P], F32, name="y")
             nc.vector.tensor_tensor(
-                y[tb][:], y_ps[tb][:].rearrange("p (a t) -> p a t", t=P), x[:, :, block_cols(tb)], ALU.add
+                y[tb][:], y_ps[tb][:].rearrange("p (a t) -> p a t", t=P), x[:, :, block(tb)], ALU.add
             )
             y_sq[tb] = norm.tile([P, CB, P], BF16, name="y_sq")
             squarer = nc.vector if tb == TB - 1 else nc.gpsimd
@@ -370,40 +371,43 @@ def tile_sequencedecodermoe_b_kernel(
                     out=y[tb][:, eb, :], in_=y[tb][:, eb, :], func=ACT.Identity,
                     bias=shift_sb[:, eb : eb + 1], scale=gain_sb[:, eb : eb + 1],
                 )
-            nc.sync.dma_start(out.rearrange("(a p) j -> p a j", p=P)[:, :, block_cols(tb)], y[tb][:])
+            nc.sync.dma_start(out.rearrange("(a p) j -> p a j", p=P)[:, :, block(tb)], y[tb][:])
 
-        for piece in range(3):
-            prepare(0, piece)
-        def block_due(n, lag):
-            steps = n - lag - STORE_LAG - (H - 1)
+        def is_item(i):
+            return 0 <= i < n_items
+
+        def block_stored(steps_ago, n):
+            steps = n - steps_ago - STORE_LAG - (H - 1)
             return steps // H if steps % H == 0 and 0 <= steps // H < TB else None
 
+        for piece in range(prepare_pieces):
+            prepare(0, piece)
         for n in range(n_items + STORE_LAG + OUT_LAG + 1):
-            if 0 <= n - STORE_LAG < n_items:
+            if is_item(n - STORE_LAG):
                 store_o(n - STORE_LAG)
-            if n < n_items - H:
+            if is_item(n + H) and n % H < prepare_pieces:
                 prepare(n // H + 1, n % H)
-            if H <= n < n_items + H and n % H == H - 1:
+            if is_item(n - H) and n % H == H - 1:
                 centre_x(n // H - 1)
-            if n < n_items:
+            if is_item(n):
                 scores(n)
             if n == 0:
                 centre_bo()
             if 1 <= n <= CB:
                 centre_wo(n - 1)
-            if 0 <= n - EXP_LAG < n_items:
-                exps(n - EXP_LAG)
-            if 0 <= n - FLIP_LAG < n_items:
+            if is_item(n - EXP_LAG):
+                exponentials(n - EXP_LAG)
+            if is_item(n - FLIP_LAG):
                 flip(n - FLIP_LAG)
-            if 0 <= n - MIX_LAG < n_items:
+            if is_item(n - MIX_LAG):
                 mix(n - MIX_LAG)
-            if 0 <= n - STORE_LAG < n_items:
+            if is_item(n - STORE_LAG):
                 project_y(n - STORE_LAG)
-            if block_due(n, PROJECT_LAG) is not None:
-                residual(block_due(n, PROJECT_LAG))
-            if block_due(n, DEVIATION_LAG) is not None:
-                deviation(block_due(n, DEVIATION_LAG))
-            if block_due(n, NORMALISE_LAG) is not None:
-                normalise(block_due(n, NORMALISE_LAG))
-            if block_due(n, OUT_LAG) is not None:
-                store_y(block_due(n, OUT_LAG))
+            if block_stored(RESIDUAL_LAG, n) is not None:
+                residual(block_stored(RESIDUAL_LAG, n))
+            if block_stored(DEVIATION_LAG, n) is not None:
+                deviation(block_stored(DEVIATION_LAG, n))
+            if block_stored(NORMALISE_LAG, n) is not None:
+                normalise(block_stored(NORMALISE_LAG, n))
+            if block_stored(OUT_LAG, n) is not None:
+                store_y(block_stored(OUT_LAG, n))

import math

import concourse.mybir as mybir
from concourse.masks import make_identity

F32 = mybir.dt.float32
BF16 = mybir.dt.bfloat16
U16 = mybir.dt.uint16
ALU = mybir.AluOpType
ACT = mybir.ActivationFunctionType
AXIS = mybir.AxisListType

P = 128
D, V, N, H = 512, 2048, 1024, 4
CB = D // P
TB = N // P
BANK = 512
PSUM_BANKS = 8
PIECE = 256
EPS = 1e-5
MASKED = -1e30

EXP_LAG, FLIP_LAG, MIX_LAG, STORE_LAG = 1, 3, 5, 6
RESIDUAL_LAG, DEVIATION_LAG, NORMALISE_LAG, OUT_LAG = 0, 2, 4, 6

FLOPS = 4 * 2 * D * D * N + 2 * 2 * D * (N * (N + 1) // 2)


def tile_sequencedecodermoe_b_kernel(
    tc, emb, pos, wq, wk, wv, wo, bq, bv, bo, gain, shift, offs, out
):
    nc = tc.nc
    with (
        tc.tile_pool(name="held", bufs=1) as held,
        tc.tile_pool(name="ring", bufs=MIX_LAG + 1) as ring,
        tc.tile_pool(name="small", bufs=MIX_LAG + 1) as small,
        tc.tile_pool(name="norm", bufs=3) as norm,
        tc.psum_pool(name="psum", bufs=PSUM_BANKS) as psum,
    ):

        def new_bank(dtype=F32, cols=BANK):
            return psum.tile([P, cols], dtype, name="bank", tag="bank")

        def block(b):
            return slice(b * P, (b + 1) * P)

        offsets = held.tile([P, N // 16], U16, name="offsets")
        nc.sync.dma_start(offsets[:], offs)

        def load_weight(w, name, queue):
            w_sb = held.tile([P, CB, D], BF16, name=name)
            queue.dma_start(w_sb[:], w.rearrange("(a p) e -> p a e", p=P))
            return w_sb

        emb_sb = [held.tile([P, V], F32, name=f"emb{c}") for c in range(CB)]
        pos_sb = [held.tile([P, N], F32, name=f"pos{c}") for c in range(CB)]
        for c in range(CB):
            nc.sync.dma_start(emb_sb[c][:], emb[block(c), :])
            nc.scalar.dma_start(pos_sb[c][:], pos[block(c), :])
            if c == 1:
                wq_sb = load_weight(wq, "wq_sb", nc.scalar)
        wk_sb = load_weight(wk, "wk_sb", nc.sync)
        wv_sb = load_weight(wv, "wv_sb", nc.sync)
        wo_sb = load_weight(wo, "wo_sb", nc.sync)

        def load_column(b, name):
            b_sb = held.tile([P, CB], F32, name=name)
            with nc.allow_non_contiguous_dma(reason="one value to a partition"):
                nc.gpsimd.dma_start(b_sb[:], b.rearrange("(a p) o -> p (a o)", p=P))
            return b_sb

        bo_sb = load_column(bo, "bo_sb")
        bq_sb = load_column(bq, "bq_sb")
        bv_sb = load_column(bv, "bv_sb")
        gain_sb = load_column(gain, "gain_sb")
        shift_sb = load_column(shift, "shift_sb")

        ident = held.tile([P, P], BF16, name="ident")
        make_identity(nc, ident[:])
        mask = held.tile([P, P], BF16, name="mask")
        nc.gpsimd.memset(mask[:], 0.0)
        nc.gpsimd.affine_select(
            out=mask[:],
            in_=mask[:],
            pattern=[[-1, P]],
            compare_op=ALU.is_ge,
            fill=MASKED,
            base=0,
            channel_multiplier=1,
        )
        averager = held.tile([P, P], BF16, name="averager")
        nc.gpsimd.memset(averager[:], 1.0 / D)
        averager_f32 = held.tile([P, P], F32, name="averager_f32")
        nc.gpsimd.memset(averager_f32[:], 1.0 / D)
        averager_col = held.tile([P, 1], BF16, name="averager_col")
        nc.gpsimd.memset(averager_col[:], 1.0 / D)
        ones_f32 = held.tile([P, P], F32, name="ones_f32")
        nc.gpsimd.memset(ones_f32[:], 1.0)
        ident_f32 = held.tile([P, P], F32, name="ident_f32")
        make_identity(nc, ident_f32[:])
        neg_half = held.tile([P, 1], F32, name="neg_half")
        nc.gpsimd.memset(neg_half[:], -0.5)

        exp_warm_up = held.tile([P, 1], F32, name="exp_warm_up")
        nc.vector.memset(exp_warm_up[:], 0.0)
        nc.scalar.activation(out=exp_warm_up[:], in_=exp_warm_up[:], func=ACT.Exp)

        x = held.tile([P, CB, N], F32, name="x")
        x_bf = held.tile([P, CB, N], BF16, name="x_bf")
        q_ps = [[new_bank() for half in range(N // BANK)] for h in range(H)]
        for c in range(CB):
            for first in range(0, N, PIECE):
                tokens = slice(first, first + PIECE)
                nc.vector.tensor_tensor(
                    x[:, c, tokens],
                    emb_sb[c][:].indirect(offsets[:, first // 16 : (first + PIECE) // 16]),
                    pos_sb[c][:, tokens],
                    ALU.add,
                )
                nc.scalar.copy(x_bf[:, c, tokens], x[:, c, tokens])
                for h in range(H):
                    nc.tensor.matmul(
                        q_ps[h][first // BANK][:, first % BANK : first % BANK + PIECE],
                        lhsT=wq_sb[:, c, block(h)],
                        rhs=x_bf[:, c, tokens],
                        start=(c == 0 and first % BANK == 0),
                        stop=(c == CB - 1 and (first + PIECE) % BANK == 0),
                    )

        x_pair_sum = held.tile([P, 2, N], F32, name="x_pair_sum")
        x_blocks_sum = held.tile([P, N], BF16, name="x_blocks_sum")
        nc.gpsimd.tensor_tensor(x_pair_sum[:, 0, :], x[:, CB - 1, :], x[:, 0, :], ALU.add)
        nc.gpsimd.tensor_tensor(x_pair_sum[:, 1, :], x[:, 1, :], x[:, 2, :], ALU.add)
        nc.gpsimd.tensor_tensor(x_blocks_sum[:], x_pair_sum[:, 0, :], x_pair_sum[:, 1, :], ALU.add)

        q_bf = held.tile([P, H, N], BF16, name="q_bf")
        for h in range(H):
            nc.vector.tensor_scalar(
                out=q_bf[:, h, 0:BANK], in0=q_ps[h][0][:], scalar1=bq_sb[:, h : h + 1], scalar2=None,
                op0=ALU.add,
            )
            nc.scalar.activation(
                out=q_bf[:, h, BANK:N], in_=q_ps[h][1][:], func=ACT.Identity,
                bias=bq_sb[:, h : h + 1], scale=1.0,
            )

        bo_centred = held.tile([P, CB], F32, name="bo_centred")
        wo_centred = held.tile([P, CB, D], BF16, name="wo_centred")

        def centre_bo():
            bo_mean_ps = new_bank()
            nc.tensor.matmul(bo_mean_ps[:, 0:CB], lhsT=averager_f32[:], rhs=bo_sb[:], start=True, stop=True)
            bo_mean = small.tile([P, 1], F32, name="bo_mean")
            nc.vector.tensor_reduce(out=bo_mean[:], in_=bo_mean_ps[:, 0:CB], axis=AXIS.X, op=ALU.add)
            nc.vector.tensor_scalar(
                out=bo_centred[:], in0=bo_sb[:], scalar1=bo_mean[:, 0:1], scalar2=None, op0=ALU.subtract
            )

        def centre_wo(c):
            row_sum = small.tile([P, 1], F32, name="wo_row_sum")
            nc.vector.tensor_reduce(out=row_sum[:], in_=wo_sb[:, c, :], axis=AXIS.X, op=ALU.add)
            neg_mean = small.tile([P, 1], F32, name="wo_neg_mean")
            nc.vector.tensor_scalar(
                out=neg_mean[:], in0=row_sum[:], scalar1=-1.0 / D, scalar2=None, op0=ALU.mult
            )
            nc.gpsimd.tensor_scalar(
                out=wo_centred[:, c, :], in0=wo_sb[:, c, :],
                scalar1=1.0, scalar2=neg_mean[:, 0:1], op0=ALU.mult, op1=ALU.add,
            )

        def centre_x(tb):
            x_mean_ps = new_bank()
            nc.tensor.matmul(
                x_mean_ps[:, 0:P], lhsT=averager[:], rhs=x_blocks_sum[:, block(tb)], start=True, stop=True
            )
            for c in range(CB):
                nc.vector.scalar_tensor_tensor(
                    out=x[:, c, block(tb)], in0=x[:, c, block(tb)], scalar=bo_centred[:, c : c + 1],
                    in1=x_mean_ps[:, 0:P], op0=ALU.add, op1=ALU.subtract,
                )

        k_bf = held.tile([P, H, N], BF16, name="k_bf")
        v_t = [held.tile([P, D], BF16, name=f"v_t{tb}") for tb in range(TB)]

        def project_k(tb, heads):
            k_ps = new_bank()
            for i, h in enumerate(heads):
                for c in range(CB):
                    nc.tensor.matmul(
                        k_ps[:, block(i)], lhsT=wk_sb[:, c, block(h)], rhs=x_bf[:, c, block(tb)],
                        start=(c == 0), stop=(c == CB - 1),
                    )
            nc.scalar.mul(
                k_bf[:, heads[0] : heads[-1] + 1, block(tb)],
                k_ps[:, 0 : len(heads) * P].rearrange("p (h t) -> p h t", t=P),
                1.0 / math.sqrt(P),
            )

        def project_v(tb):
            v_ps = new_bank()
            for c in range(CB):
                nc.tensor.matmul(
                    v_ps[:], lhsT=x_bf[:, c, block(tb)], rhs=wv_sb[:, c, :],
                    start=(c == 0), stop=(c == CB - 1),
                )
            nc.scalar.copy(v_t[tb][:], v_ps[:])

        def prepare(tb, piece):
            if piece == 0:
                project_k(tb, [0, 1])
            elif piece == 1:
                project_k(tb, [2, 3])
            else:
                project_v(tb)

        prepare_pieces = 3

        items = [(jb, h) for jb in range(TB) for h in range(H)]
        n_items = len(items)
        score_ps = [None] * n_items
        neg_max = [None] * n_items
        prob = [None] * n_items
        diag_r = [None] * n_items
        weights_t = [None] * n_items
        o_ps = [None] * n_items
        o_bf = held.tile([P, H, N], BF16, name="o_bf")

        def key_starts(jb):
            return list(range(0, (jb + 1) * P, BANK))

        def scores(n):
            jb, h = items[n]
            keys = (jb + 1) * P
            banks = []
            for a in key_starts(jb):
                b = min(a + BANK, keys)
                s_ps = new_bank()
                past = min(b, jb * P)
                if past > a:
                    nc.tensor.matmul(
                        s_ps[:, 0 : past - a], lhsT=q_bf[:, h, block(jb)], rhs=k_bf[:, h, a:past],
                        start=True, stop=True,
                    )
                if b == keys:
                    own = s_ps[:, jb * P - a : keys - a]
                    nc.tensor.matmul(
                        own, lhsT=q_bf[:, h, block(jb)], rhs=k_bf[:, h, block(jb)], start=True, stop=False
                    )
                    nc.tensor.matmul(own, lhsT=ident[:], rhs=mask[:], start=False, stop=True)
                banks.append(s_ps)
            score_ps[n] = banks
            parts = small.tile([P, len(banks)], F32, name="neg_max_parts")
            for i, a in enumerate(key_starts(jb)):
                nc.vector.tensor_reduce(
                    out=parts[:, i : i + 1], in_=banks[i][:, 0 : min(BANK, keys - a)],
                    axis=AXIS.X, op=ALU.max, negate=True,
                )
            if len(banks) == 1:
                neg_max[n] = parts
            else:
                neg_max[n] = small.tile([P, 1], F32, name="neg_max")
                nc.vector.tensor_reduce(out=neg_max[n][:], in_=parts[:], axis=AXIS.X, op=ALU.min)

        def exponentials(n):
            jb, h = items[n]
            keys = (jb + 1) * P
            banks = score_ps[n]
            prob[n] = ring.tile([P, N], BF16, name="prob")
            parts = small.tile([P, len(banks)], F32, name="sum_parts")
            for i, a in enumerate(key_starts(jb)):
                b = min(a + BANK, keys)
                nc.scalar.activation(
                    out=prob[n][:, a:b], in_=banks[i][:, 0 : b - a], func=ACT.Exp,
                    bias=neg_max[n][:, 0:1], scale=1.0, accum_out=parts[:, i : i + 1],
                )
            if len(banks) == 1:
                total = parts
            else:
                total = small.tile([P, 1], F32, name="total")
                nc.scalar.activation(
                    out=total[:], in_=parts[:, 0:1], func=ACT.Identity, bias=parts[:, 1:2], scale=1.0
                )
            recip = small.tile([P, 1], F32, name="recip")
            nc.vector.reciprocal(recip[:], total[:, 0:1])
            diag_r[n] = ring.tile([P, P], BF16, name="diag_r")
            nc.scalar.activation(out=diag_r[n][:], in_=ident[:], func=ACT.Identity, scale=recip[:, 0:1])

        def flip(n):
            jb, h = items[n]
            keys = (jb + 1) * P
            t_ps = new_bank(BF16, 2 * BANK)
            for tb in range(jb + 1):
                nc.tensor.matmul(
                    t_ps[:, block(tb)], lhsT=prob[n][:, block(tb)], rhs=diag_r[n][:], start=True, stop=True
                )
            weights_t[n] = ring.tile([P, N], BF16, name="weights_t")
            if h < H - 1:
                nc.vector.tensor_copy(weights_t[n][:, 0:keys], t_ps[:, 0:keys])
            else:
                nc.scalar.copy(weights_t[n][:, 0:keys], t_ps[:, 0:keys])

        def mix(n):
            jb, h = items[n]
            o_ps[n] = new_bank()
            for tb in range(jb + 1):
                nc.tensor.matmul(
                    o_ps[n][:, 0:P], lhsT=v_t[tb][:, block(h)], rhs=weights_t[n][:, block(tb)],
                    start=(tb == 0), stop=(tb == jb),
                )

        def store_o(n):
            jb, h = items[n]
            nc.scalar.activation(
                out=o_bf[:, h, block(jb)], in_=o_ps[n][:, 0:P], func=ACT.Identity,
                bias=bv_sb[:, h : h + 1], scale=1.0,
            )

        y_ps = [None] * TB
        y = [None] * TB
        y_sq = [None] * TB
        rstd_rows = [None] * TB

        def project_y(n):
            tb, h = items[n]
            if h == 0:
                y_ps[tb] = new_bank()
            for eb in range(CB):
                nc.tensor.matmul(
                    y_ps[tb][:, block(eb)], lhsT=wo_centred[:, h, block(eb)], rhs=o_bf[:, h, block(tb)],
                    start=(h == 0 and eb == 0), stop=(h == H - 1 and eb == CB - 1),
                )

        def residual(tb):
            y[tb] = norm.tile([P, CB, P], F32, name="y")
            nc.vector.tensor_tensor(
                y[tb][:], y_ps[tb][:].rearrange("p (a t) -> p a t", t=P), x[:, :, block(tb)], ALU.add
            )
            y_sq[tb] = norm.tile([P, CB, P], BF16, name="y_sq")
            squarer = nc.vector if tb == TB - 1 else nc.gpsimd
            squarer.tensor_tensor(y_sq[tb][:], y[tb][:], y[tb][:], ALU.mult)

        def deviation(tb):
            var_ps = new_bank()
            for eb in range(CB):
                nc.tensor.matmul(
                    var_ps[:, 0:1], lhsT=y_sq[tb][:, eb, :], rhs=averager_col[:],
                    start=(eb == 0), stop=(eb == CB - 1),
                )
            var_eps = small.tile([P, 1], F32, name="var_eps")
            nc.vector.tensor_scalar(
                out=var_eps[:], in0=var_ps[:, 0:1], scalar1=EPS, scalar2=None, op0=ALU.add
            )
            rstd = small.tile([P, 1], F32, name="rstd")
            nc.gpsimd.tensor_tensor(rstd[:], var_eps[:], neg_half[:], ALU.pow)
            rstd_rows[tb] = norm.tile([P, P], F32, name="rstd_rows")
            nc.gpsimd.tensor_scalar(
                out=rstd_rows[tb][:], in0=ones_f32[:], scalar1=rstd[:, 0:1], scalar2=0.0,
                op0=ALU.mult, op1=ALU.add,
            )

        def normalise(tb):
            rstd_ps = new_bank()
            nc.tensor.transpose(rstd_ps[:, 0:P], rstd_rows[tb][:], ident_f32[:])
            nc.vector.tensor_tensor(
                y[tb][:], y[tb][:], rstd_ps[:, 0:P].unsqueeze(1).to_broadcast([P, CB, P]), ALU.mult
            )

        def store_y(tb):
            for eb in range(CB):
                nc.scalar.activation(
                    out=y[tb][:, eb, :], in_=y[tb][:, eb, :], func=ACT.Identity,
                    bias=shift_sb[:, eb : eb + 1], scale=gain_sb[:, eb : eb + 1],
                )
            nc.sync.dma_start(out.rearrange("(a p) j -> p a j", p=P)[:, :, block(tb)], y[tb][:])

        def is_item(i):
            return 0 <= i < n_items

        def block_stored(steps_ago, n):
            steps = n - steps_ago - STORE_LAG - (H - 1)
            return steps // H if steps % H == 0 and 0 <= steps // H < TB else None

        for piece in range(prepare_pieces):
            prepare(0, piece)
        for n in range(n_items + STORE_LAG + OUT_LAG + 1):
            if is_item(n - STORE_LAG):
                store_o(n - STORE_LAG)
            if is_item(n + H) and n % H < prepare_pieces:
                prepare(n // H + 1, n % H)
            if is_item(n - H) and n % H == H - 1:
                centre_x(n // H - 1)
            if is_item(n):
                scores(n)
            if n == 0:
                centre_bo()
            if 1 <= n <= CB:
                centre_wo(n - 1)
            if is_item(n - EXP_LAG):
                exponentials(n - EXP_LAG)
            if is_item(n - FLIP_LAG):
                flip(n - FLIP_LAG)
            if is_item(n - MIX_LAG):
                mix(n - MIX_LAG)
            if is_item(n - STORE_LAG):
                project_y(n - STORE_LAG)
            if block_stored(RESIDUAL_LAG, n) is not None:
                residual(block_stored(RESIDUAL_LAG, n))
            if block_stored(DEVIATION_LAG, n) is not None:
                deviation(block_stored(DEVIATION_LAG, n))
            if block_stored(NORMALISE_LAG, n) is not None:
                normalise(block_stored(NORMALISE_LAG, n))
            if block_stored(OUT_LAG, n) is not None:
                store_y(block_stored(OUT_LAG, n))
